import numpy as np
import ml_dtypes


def mxq(x, axis, fmt="e4m3"):
    dtype, down = {"e4m3": (ml_dtypes.float8_e4m3fn, 7), "e5m2": (ml_dtypes.float8_e5m2, 14)}[fmt]
    v = np.moveaxis(np.asarray(x, np.float32).astype(ml_dtypes.bfloat16).astype(np.float64), axis, -1)
    blocks = v.reshape(v.shape[:-1] + (-1, 32))
    amax = np.abs(blocks).max(-1, keepdims=True)
    byte = np.maximum(np.where(amax > 0, np.frexp(amax)[1] - 1 + 127, 0) - down, 1)
    scale = np.exp2(byte - 127.0)
    codes = (blocks / scale).astype(np.float32).astype(dtype).astype(np.float64)
    return np.moveaxis((codes * scale).reshape(v.shape), -1, axis)


WIDE = False


def mx_kscale(k):
    if not WIDE:
        return np.ones(k)
    levels = np.array([10, -10, 5, -5, 0])
    a = np.random.permutation(np.resize(levels, k // 512 * 4)).reshape(k // 512, 4)
    idx = np.arange(k)
    return np.exp2(a[idx // 512, idx % 128 // 32])


BF16 = ml_dtypes.bfloat16


def bf(x):
    return np.asarray(x, np.float32).astype(BF16)


def f64(x):
    return np.asarray(x).astype(np.float64)


E2M1 = np.array([0.0, 0.5, 1.0, 1.5, 2.0, 3.0, 4.0, 6.0, -0.0, -0.5, -1.0, -1.5, -2.0, -3.0, -4.0, -6.0])


def pack_weight(w, fmt):
    k, n = w.shape
    w = f64(bf(w)).reshape(k // 32, 32, n)
    amax = np.abs(w).max(1)
    if fmt == "e4m3":
        byte = np.frexp(amax)[1] - 1 + 127 - 7
    else:
        mant, ex = np.frexp(amax / 6.0)
        byte = np.where(mant > 0.5, ex, ex - 1) + 127
    byte = np.clip(np.where(amax > 0, byte, 1), 1, 254)
    scaled = (w * np.exp2(127.0 - byte)[:, None, :]).reshape(k, n).astype(np.float32)
    by_word = np.ascontiguousarray(scaled.reshape(k // 512, 128, 4, n).transpose(0, 1, 3, 2))
    if fmt == "e4m3":
        words = by_word.astype(ml_dtypes.float8_e4m3fn).view(np.uint8)
    else:
        c = by_word.astype(ml_dtypes.float4_e2m1fn).view(np.uint8) & 0xF
        words = c[..., 0::2] | (c[..., 1::2] << 4)
    return np.ascontiguousarray(words), np.ascontiguousarray(byte.astype(np.uint8).reshape(k // 512, 16, n))


def unpack_weight(words, scales, fmt):
    g, p, n, _ = words.shape
    if fmt == "e4m3":
        vals = np.ascontiguousarray(words).view(ml_dtypes.float8_e4m3fn).astype(np.float64)
    else:
        nib = np.empty((g, p, n, 4), np.uint8)
        nib[..., 0::2] = words & 0xF
        nib[..., 1::2] = words >> 4
        vals = E2M1[nib]
    vals = vals * np.repeat(np.exp2(scales.astype(np.float64) - 127.0), 8, axis=1)[..., None]
    return vals.transpose(0, 1, 3, 2).reshape(g * 512, n)

def pack4(w):
    words, scales = pack_weight(w, "e2m1")
    return words.reshape(words.shape[0], 128, -1), scales


def unpack4(words, scales):
    return unpack_weight(words.reshape(words.shape[0], 128, -1, 2), scales, "e2m1")


B, S, HID, H, D = 4, 2048, 512, 2, 64
QKV = 3 * H * D


def rotate_half(x):
    x1, x2 = x[..., : x.shape[-1] // 2], x[..., x.shape[-1] // 2 :]
    return np.concatenate((-x2, x1), axis=-1)


def setup_inputs():
    s = mx_kscale(HID)
    hidden_states = bf(np.random.standard_normal((B, S, HID)) * s)
    cos = bf(np.random.uniform(size=(S, D)))
    sin = bf(np.random.uniform(size=(S, D)))
    words, scales = pack4(np.random.standard_normal((HID, QKV)) * 2.0 / np.sqrt(HID) / s[:, None])
    return {"hidden_states": hidden_states,
            "cos": cos,
            "sin": sin,
            "w_qkv_words": words,
            "w_qkv_scales": scales}


def reference(hidden_states, cos, sin, w_qkv_words, w_qkv_scales):
    qkv = mxq(f64(hidden_states), 2, "e4m3") @ unpack4(w_qkv_words, w_qkv_scales)
    qkv = qkv.reshape(B, S, 3 * H, D)
    q, k, v = qkv[:, :, :H], qkv[:, :, H:2 * H], qkv[:, :, 2 * H:]
    c = f64(cos)[:, None, :]
    sn = f64(sin)[:, None, :]
    q_rot = q * c + rotate_half(q) * sn
    k_rot = k * c + rotate_half(k) * sn
    return q_rot, k_rot, v

@@ -1,0 +1,223 @@
+from contextlib import ExitStack
+
+import concourse.mybir as mybir
+from concourse.masks import make_identity
+
+F32 = mybir.dt.float32
+BF16 = mybir.dt.bfloat16
+I32 = mybir.dt.int32
+U32 = mybir.dt.uint32
+U8 = mybir.dt.uint8
+FP8X4 = mybir.dt.float8_e4m3fn_x4
+FP4X4 = mybir.dt.float4_e2m1fn_x4
+MULT = mybir.AluOpType.mult
+ADD = mybir.AluOpType.add
+
+P = 128
+BATCH, SEQ, HID = 4, 2048, 512
+HEAD = 64
+HALF = HEAD // 2
+QK_HEADS = 4
+QK = QK_HEADS * HEAD
+V = 2 * HEAD
+ROWS = SEQ // P
+TILES = 4
+GROUPS = BATCH * ROWS // TILES
+
+FLOPS = 2 * BATCH * SEQ * HID * (QK + V)
+
+LOAD_AHEAD = 5
+TRANSPOSE_AHEAD = 3
+QUANTISE_AHEAD = 2
+VECTOR_ADDS = 1
+
+
+def tile_attention_pa_t_kernel(
+    tc, hidden_states, cos, sin, w_qkv_words, w_qkv_scales, out_0, out_1, out_2
+):
+    nc = tc.nc
+    x_hbm = hidden_states.rearrange("b (p j) k -> b p j k", j=ROWS)
+    q_hbm = out_0.rearrange("b (p j) h d -> b p j (h d)", j=ROWS)
+    k_hbm = out_1.rearrange("b (p j) h d -> b p j (h d)", j=ROWS)
+    v_hbm = out_2.rearrange("b (p j) h d -> b p j (h d)", j=ROWS)
+
+    with ExitStack() as stack:
+        consts = stack.enter_context(tc.tile_pool(name="consts", bufs=1))
+        x_pool = stack.enter_context(tc.tile_pool(name="x", bufs=LOAD_AHEAD))
+        grouped_pool = stack.enter_context(tc.tile_pool(name="grouped", bufs=3))
+        mx_pool = stack.enter_context(tc.tile_pool(name="mx", bufs=3))
+        product_pool = stack.enter_context(tc.tile_pool(name="products", bufs=3))
+        out_pool = stack.enter_context(tc.tile_pool(name="outputs", bufs=4))
+        xt_psum = stack.enter_context(tc.psum_pool(name="xt", bufs=2))
+        qk_psum = stack.enter_context(tc.psum_pool(name="qk", bufs=4))
+        v_psum = stack.enter_context(tc.psum_pool(name="v", bufs=2))
+        stack.enter_context(tc.manual_schedule())
+
+        x_tiles, xt_tiles, grouped_tiles, code_tiles, scale_tiles = {}, {}, {}, {}, {}
+        qk_banks, v_banks, product_tiles, qk_outs, v_outs = {}, {}, {}, {}, {}
+
+        def where(g):
+            return g // (ROWS // TILES), TILES * (g % (ROWS // TILES))
+
+        def load(g):
+            b, j0 = where(g)
+            x_tile = x_pool.tile([P, TILES, HID], BF16)
+            nc.sync.dma_start(out=x_tile[:], in_=x_hbm[b, :, j0 : j0 + TILES, :])
+            x_tiles[g] = x_tile
+
+        identity = consts.tile([P, P], F32)
+        make_identity(nc, identity[:])
+
+        w_words = consts.tile([P, 2 * (QK + V)], U8, align_bytes=64)
+        w_scales = consts.tile([P, QK + V], U8, align_bytes=64)
+        nc.vector.memset(w_scales[:].bitcast(I32), 0)
+        tables = consts.tile([P, 2, ROWS, HEAD], BF16)
+
+        load(0)
+        nc.sync.dma_start(out=w_words[:].bitcast(I32), in_=w_qkv_words[0].bitcast(I32))
+        for quadrant in range(4):
+            nc.sync.dma_start(
+                out=w_scales[32 * quadrant : 32 * quadrant + 4, :].bitcast(I32),
+                in_=w_qkv_scales[0, 4 * quadrant : 4 * quadrant + 4, :].bitcast(I32),
+            )
+        nc.sync.dma_start(out=tables[:, 0, :, :], in_=cos.rearrange("(p j) d -> p j d", j=ROWS))
+        nc.sync.dma_start(out=tables[:, 1, :, :], in_=sin.rearrange("(p j) d -> p j d", j=ROWS))
+        for g in range(1, LOAD_AHEAD):
+            load(g)
+
+        w_words_swapped = consts.tile([P, 2 * QK], U8, align_bytes=64)
+        w_scales_swapped = consts.tile([P, QK], U8, align_bytes=64)
+
+        def exchange_halves(dst, src):
+            dst_halves = dst.bitcast(I32).rearrange("p (h two w) -> p h two w", h=QK_HEADS, two=2)
+            src_halves = src.bitcast(I32).rearrange("p (h two w) -> p h two w", h=QK_HEADS, two=2)
+            nc.vector.tensor_copy(out=dst_halves[:, :, 0, :], in_=src_halves[:, :, 1, :])
+            nc.vector.tensor_copy(out=dst_halves[:, :, 1, :], in_=src_halves[:, :, 0, :])
+
+        exchange_halves(w_words_swapped[:], w_words[:, 0 : 2 * QK])
+        exchange_halves(w_scales_swapped[:], w_scales[:, 0:QK])
+
+        nc.vector.tensor_scalar(
+            out=tables[:, 1, :, 0:HALF],
+            in0=tables[:, 1, :, 0:HALF],
+            scalar1=-1.0,
+            scalar2=None,
+            op0=MULT,
+        )
+
+        def transpose(g):
+            x_words = x_tiles[g][:].bitcast(F32)
+            xt_tiles[g] = []
+            for pair in range(TILES // 2):
+                x_transposed = xt_psum.tile([P, 2, 2, P], F32)
+                for t in range(2):
+                    for u in range(2):
+                        nc.tensor.transpose(
+                            x_transposed[:, t, u, :],
+                            x_words[:, 2 * pair + t, u : HID // 2 : 2],
+                            identity[:],
+                        )
+                xt_tiles[g].append(x_transposed)
+
+        def regroup(g):
+            grouped = grouped_pool.tile([P, TILES * P * 4], BF16, align_bytes=64)
+            grouped_words = grouped[:].bitcast(F32).rearrange(
+                "p (t r u) -> p t r u", t=TILES, u=2
+            )
+            for pair in range(TILES // 2):
+                nc.scalar.copy(
+                    out=grouped_words[:, 2 * pair : 2 * pair + 2, :, :],
+                    in_=xt_tiles[g][pair][:].rearrange("p t u r -> p t r u"),
+                )
+            grouped_tiles[g] = grouped
+
+        def quantise(g):
+            codes = mx_pool.tile([P, TILES * P], U32, align_bytes=64)
+            scales = mx_pool.tile([P, TILES * P], U8, align_bytes=64)
+            nc.vector.quantize_mx(
+                out=codes[:].bitcast(FP8X4), scales=scales[:], in_=grouped_tiles[g][:]
+            )
+            code_tiles[g], scale_tiles[g] = codes, scales
+
+        def project(g):
+            v_bank = v_psum.tile([P, TILES, V], F32)
+            qk_banks[g] = []
+            for t in range(TILES):
+                tokens = slice(P * t, P * (t + 1))
+                qk_bank = qk_psum.tile([P, 2 * QK], F32)
+
+                def multiply(out, words, scales):
+                    nc.tensor.matmul_mx(
+                        out=out,
+                        lhsT=code_tiles[g][:, tokens].bitcast(FP8X4),
+                        lhsT_scale=scale_tiles[g][:, tokens],
+                        rhs=words.bitcast(FP4X4),
+                        rhs_scale=scales,
+                        start=True,
+                        stop=True,
+                    )
+
+                multiply(qk_bank[:, 0:QK], w_words[:, 0 : 2 * QK], w_scales[:, 0:QK])
+                multiply(qk_bank[:, QK : 2 * QK], w_words_swapped[:], w_scales_swapped[:])
+                multiply(v_bank[:, t, :], w_words[:, 2 * QK :], w_scales[:, QK:])
+                qk_banks[g].append(qk_bank)
+            v_banks[g] = v_bank
+            products = product_pool.tile([P, TILES, 2 * QK], F32)
+            product_tiles[g] = products
+            qk_out = out_pool.tile([P, 2, TILES, 2 * HEAD], F32)
+            qk_outs[g] = qk_out
+
+        def rotate(g, t):
+            j = where(g)[1] + t
+            nc.vector.tensor_tensor(
+                out=product_tiles[g][:, t, :].rearrange("p (c h d) -> p c h d", c=2, h=QK_HEADS),
+                in0=qk_banks[g][t][:].rearrange("p (c h d) -> p c h d", c=2, h=QK_HEADS),
+                in1=tables[:, :, j, :].unsqueeze(2).to_broadcast([P, 2, QK_HEADS, HEAD]),
+                op=MULT,
+            )
+
+        def add(engine, g, first, last):
+            products = product_tiles[g][:, first:last, :]
+            engine.tensor_tensor(
+                out=qk_outs[g][:, :, first:last, :].rearrange("p a t n -> p t a n"),
+                in0=products[:, :, 0:QK].rearrange("p t (a n) -> p t a n", a=2),
+                in1=products[:, :, QK : 2 * QK].rearrange("p t (a n) -> p t a n", a=2),
+                op=ADD,
+            )
+
+        def copy_v(g):
+            v_out = out_pool.tile([P, TILES, V], F32)
+            nc.scalar.copy(out=v_out[:], in_=v_banks[g][:])
+            v_outs[g] = v_out
+
+        def store(g):
+            b, j0 = where(g)
+            rows = slice(j0, j0 + TILES)
+            nc.sync.dma_start(out=v_hbm[b, :, rows, :], in_=v_outs[g][:])
+            nc.sync.dma_start(out=q_hbm[b, :, rows, :], in_=qk_outs[g][:, 0, :, :])
+            nc.sync.dma_start(out=k_hbm[b, :, rows, :], in_=qk_outs[g][:, 1, :, :])
+
+        for g in range(TRANSPOSE_AHEAD):
+            transpose(g)
+            regroup(g)
+            if g < QUANTISE_AHEAD:
+                quantise(g)
+
+        for g in range(GROUPS):
+            if g + LOAD_AHEAD < GROUPS:
+                load(g + LOAD_AHEAD)
+            project(g)
+            copy_v(g)
+            if g + TRANSPOSE_AHEAD < GROUPS:
+                transpose(g + TRANSPOSE_AHEAD)
+                regroup(g + TRANSPOSE_AHEAD)
+            for t in range(TILES - 1):
+                rotate(g, t)
+            add(nc.vector, g, 0, VECTOR_ADDS)
+            if g + QUANTISE_AHEAD < GROUPS:
+                quantise(g + QUANTISE_AHEAD)
+            rotate(g, TILES - 1)
+            add(nc.gpsimd, g, VECTOR_ADDS, TILES)
+            if g >= 1:
+                store(g - 1)
+        store(GROUPS - 1)

@@ -28,8 +28,6 @@ FLOPS = 2 * BATCH * SEQ * HID * (QK + V)
 
 LOAD_AHEAD = 5
 TRANSPOSE_AHEAD = 3
-QUANTISE_AHEAD = 2
-VECTOR_ADDS = 1
 
 
 def tile_attention_pa_t_kernel(
@@ -44,17 +42,17 @@ def tile_attention_pa_t_kernel(
     with ExitStack() as stack:
         consts = stack.enter_context(tc.tile_pool(name="consts", bufs=1))
         x_pool = stack.enter_context(tc.tile_pool(name="x", bufs=LOAD_AHEAD))
-        grouped_pool = stack.enter_context(tc.tile_pool(name="grouped", bufs=3))
-        mx_pool = stack.enter_context(tc.tile_pool(name="mx", bufs=3))
+        grouped_pool = stack.enter_context(tc.tile_pool(name="grouped", bufs=4))
+        mx_pool = stack.enter_context(tc.tile_pool(name="mx", bufs=4))
         product_pool = stack.enter_context(tc.tile_pool(name="products", bufs=3))
-        out_pool = stack.enter_context(tc.tile_pool(name="outputs", bufs=4))
+        out_pool = stack.enter_context(tc.tile_pool(name="outputs", bufs=3))
         xt_psum = stack.enter_context(tc.psum_pool(name="xt", bufs=2))
         qk_psum = stack.enter_context(tc.psum_pool(name="qk", bufs=4))
         v_psum = stack.enter_context(tc.psum_pool(name="v", bufs=2))
         stack.enter_context(tc.manual_schedule())
 
         x_tiles, xt_tiles, grouped_tiles, code_tiles, scale_tiles = {}, {}, {}, {}, {}
-        qk_banks, v_banks, product_tiles, qk_outs, v_outs = {}, {}, {}, {}, {}
+        qk_banks, v_banks = {}, {}
 
         def where(g):
             return g // (ROWS // TILES), TILES * (g % (ROWS // TILES))
@@ -162,62 +160,72 @@ def tile_attention_pa_t_kernel(
                 multiply(v_bank[:, t, :], w_words[:, 2 * QK :], w_scales[:, QK:])
                 qk_banks[g].append(qk_bank)
             v_banks[g] = v_bank
-            products = product_pool.tile([P, TILES, 2 * QK], F32)
-            product_tiles[g] = products
-            qk_out = out_pool.tile([P, 2, TILES, 2 * HEAD], F32)
-            qk_outs[g] = qk_out
 
-        def rotate(g, t):
+        def store_v(g):
+            b, j0 = where(g)
+            v_out = out_pool.tile([P, TILES, V], F32)
+            nc.scalar.copy(out=v_out[:], in_=v_banks[g][:])
+            nc.sync.dma_start(out=v_hbm[b, :, j0 : j0 + TILES, :], in_=v_out[:])
+
+        def feed(g):
+            if g + LOAD_AHEAD < GROUPS:
+                load(g + LOAD_AHEAD)
+            project(g)
+            store_v(g)
+            if g + TRANSPOSE_AHEAD < GROUPS:
+                transpose(g + TRANSPOSE_AHEAD)
+                regroup(g + TRANSPOSE_AHEAD)
+
+        def rotate(products, i, g, t):
             j = where(g)[1] + t
             nc.vector.tensor_tensor(
-                out=product_tiles[g][:, t, :].rearrange("p (c h d) -> p c h d", c=2, h=QK_HEADS),
+                out=products[:, i, :].rearrange("p (c h d) -> p c h d", c=2, h=QK_HEADS),
                 in0=qk_banks[g][t][:].rearrange("p (c h d) -> p c h d", c=2, h=QK_HEADS),
                 in1=tables[:, :, j, :].unsqueeze(2).to_broadcast([P, 2, QK_HEADS, HEAD]),
                 op=MULT,
             )
 
-        def add(engine, g, first, last):
-            products = product_tiles[g][:, first:last, :]
+        def add(engine, products, qk_out, first, last):
             engine.tensor_tensor(
-                out=qk_outs[g][:, :, first:last, :].rearrange("p a t n -> p t a n"),
-                in0=products[:, :, 0:QK].rearrange("p t (a n) -> p t a n", a=2),
-                in1=products[:, :, QK : 2 * QK].rearrange("p t (a n) -> p t a n", a=2),
+                out=qk_out[:, :, first:last, :].rearrange("p a i n -> p i a n"),
+                in0=products[:, first:last, 0:QK].rearrange("p i (a n) -> p i a n", a=2),
+                in1=products[:, first:last, QK : 2 * QK].rearrange("p i (a n) -> p i a n", a=2),
                 op=ADD,
             )
 
-        def copy_v(g):
-            v_out = out_pool.tile([P, TILES, V], F32)
-            nc.scalar.copy(out=v_out[:], in_=v_banks[g][:])
-            v_outs[g] = v_out
-
-        def store(g):
-            b, j0 = where(g)
-            rows = slice(j0, j0 + TILES)
-            nc.sync.dma_start(out=v_hbm[b, :, rows, :], in_=v_outs[g][:])
-            nc.sync.dma_start(out=q_hbm[b, :, rows, :], in_=qk_outs[g][:, 0, :, :])
-            nc.sync.dma_start(out=k_hbm[b, :, rows, :], in_=qk_outs[g][:, 1, :, :])
+        def store_qk(groups, qk_out):
+            for n, g in enumerate(groups):
+                b, j0 = where(g)
+                tiles = slice(TILES * n, TILES * (n + 1))
+                nc.sync.dma_start(out=q_hbm[b, :, j0 : j0 + TILES, :], in_=qk_out[:, 0, tiles, :])
+                nc.sync.dma_start(out=k_hbm[b, :, j0 : j0 + TILES, :], in_=qk_out[:, 1, tiles, :])
 
         for g in range(TRANSPOSE_AHEAD):
             transpose(g)
             regroup(g)
-            if g < QUANTISE_AHEAD:
-                quantise(g)
+        quantise(0)
 
-        for g in range(GROUPS):
-            if g + LOAD_AHEAD < GROUPS:
-                load(g + LOAD_AHEAD)
-            project(g)
-            copy_v(g)
-            if g + TRANSPOSE_AHEAD < GROUPS:
-                transpose(g + TRANSPOSE_AHEAD)
-                regroup(g + TRANSPOSE_AHEAD)
-            for t in range(TILES - 1):
-                rotate(g, t)
-            add(nc.vector, g, 0, VECTOR_ADDS)
-            if g + QUANTISE_AHEAD < GROUPS:
-                quantise(g + QUANTISE_AHEAD)
-            rotate(g, TILES - 1)
-            add(nc.gpsimd, g, VECTOR_ADDS, TILES)
-            if g >= 1:
-                store(g - 1)
-        store(GROUPS - 1)
+        rounds = [range(0, 1)]
+        rounds += [range(g, g + 2) for g in range(1, GROUPS - 1, 2)]
+        rounds += [range(GROUPS - 1, GROUPS)]
+        waiting = None
+        for r, groups in enumerate(rounds):
+            following = rounds[r + 1] if r + 1 < len(rounds) else range(0)
+            tiles = [(g, t) for g in groups for t in range(TILES)]
+            count = len(tiles)
+            early = count - (min(len(groups), max(len(following), 1)) * TILES - 2)
+            products = product_pool.tile([P, count, 2 * QK], F32)
+            qk_out = out_pool.tile([P, 2, count, 2 * HEAD], F32)
+            for i, (g, t) in enumerate(tiles):
+                if t == 0:
+                    feed(g)
+                if i == count - 1:
+                    add(nc.vector, products, qk_out, 0, early)
+                    for ahead in following:
+                        quantise(ahead)
+                rotate(products, i, g, t)
+            add(nc.gpsimd if len(following) > 0 else nc.vector, products, qk_out, early, count)
+            if waiting is not None:
+                store_qk(*waiting)
+            waiting = (groups, qk_out)
+        store_qk(*waiting)

@@ -26,7 +26,6 @@ GROUPS = BATCH * ROWS // TILES
 
 FLOPS = 2 * BATCH * SEQ * HID * (QK + V)
 
-LOAD_AHEAD = 5
 TRANSPOSE_AHEAD = 3
 
 
@@ -41,11 +40,11 @@ def tile_attention_pa_t_kernel(
 
     with ExitStack() as stack:
         consts = stack.enter_context(tc.tile_pool(name="consts", bufs=1))
-        x_pool = stack.enter_context(tc.tile_pool(name="x", bufs=LOAD_AHEAD))
+        x_pool = stack.enter_context(tc.tile_pool(name="x", bufs=GROUPS))
         grouped_pool = stack.enter_context(tc.tile_pool(name="grouped", bufs=4))
         mx_pool = stack.enter_context(tc.tile_pool(name="mx", bufs=4))
         product_pool = stack.enter_context(tc.tile_pool(name="products", bufs=3))
-        out_pool = stack.enter_context(tc.tile_pool(name="outputs", bufs=3))
+        out_pool = stack.enter_context(tc.tile_pool(name="outputs", bufs=6))
         xt_psum = stack.enter_context(tc.psum_pool(name="xt", bufs=2))
         qk_psum = stack.enter_context(tc.psum_pool(name="qk", bufs=4))
         v_psum = stack.enter_context(tc.psum_pool(name="v", bufs=2))
@@ -80,7 +79,7 @@ def tile_attention_pa_t_kernel(
             )
         nc.sync.dma_start(out=tables[:, 0, :, :], in_=cos.rearrange("(p j) d -> p j d", j=ROWS))
         nc.sync.dma_start(out=tables[:, 1, :, :], in_=sin.rearrange("(p j) d -> p j d", j=ROWS))
-        for g in range(1, LOAD_AHEAD):
+        for g in range(1, GROUPS):
             load(g)
 
         w_words_swapped = consts.tile([P, 2 * QK], U8, align_bytes=64)
@@ -168,8 +167,6 @@ def tile_attention_pa_t_kernel(
             nc.sync.dma_start(out=v_hbm[b, :, j0 : j0 + TILES, :], in_=v_out[:])
 
         def feed(g):
-            if g + LOAD_AHEAD < GROUPS:
-                load(g + LOAD_AHEAD)
             project(g)
             store_v(g)
             if g + TRANSPOSE_AHEAD < GROUPS:

@@ -46,8 +46,7 @@ def tile_attention_pa_t_kernel(
         product_pool = stack.enter_context(tc.tile_pool(name="products", bufs=3))
         out_pool = stack.enter_context(tc.tile_pool(name="outputs", bufs=6))
         xt_psum = stack.enter_context(tc.psum_pool(name="xt", bufs=2))
-        qk_psum = stack.enter_context(tc.psum_pool(name="qk", bufs=4))
-        v_psum = stack.enter_context(tc.psum_pool(name="v", bufs=2))
+        qkv_psum = stack.enter_context(tc.psum_pool(name="qkv", bufs=2))
         stack.enter_context(tc.manual_schedule())
 
         x_tiles, xt_tiles, grouped_tiles, code_tiles, scale_tiles = {}, {}, {}, {}, {}
@@ -69,6 +68,7 @@ def tile_attention_pa_t_kernel(
         w_scales = consts.tile([P, QK + V], U8, align_bytes=64)
         nc.vector.memset(w_scales[:].bitcast(I32), 0)
         tables = consts.tile([P, 2, ROWS, HEAD], BF16)
+        sin_rows = consts.tile([P, ROWS, HEAD], BF16)
 
         load(0)
         nc.sync.dma_start(out=w_words[:].bitcast(I32), in_=w_qkv_words[0].bitcast(I32))
@@ -78,25 +78,14 @@ def tile_attention_pa_t_kernel(
                 in_=w_qkv_scales[0, 4 * quadrant : 4 * quadrant + 4, :].bitcast(I32),
             )
         nc.sync.dma_start(out=tables[:, 0, :, :], in_=cos.rearrange("(p j) d -> p j d", j=ROWS))
-        nc.sync.dma_start(out=tables[:, 1, :, :], in_=sin.rearrange("(p j) d -> p j d", j=ROWS))
+        nc.sync.dma_start(out=sin_rows[:], in_=sin.rearrange("(p j) d -> p j d", j=ROWS))
         for g in range(1, GROUPS):
             load(g)
 
-        w_words_swapped = consts.tile([P, 2 * QK], U8, align_bytes=64)
-        w_scales_swapped = consts.tile([P, QK], U8, align_bytes=64)
-
-        def exchange_halves(dst, src):
-            dst_halves = dst.bitcast(I32).rearrange("p (h two w) -> p h two w", h=QK_HEADS, two=2)
-            src_halves = src.bitcast(I32).rearrange("p (h two w) -> p h two w", h=QK_HEADS, two=2)
-            nc.vector.tensor_copy(out=dst_halves[:, :, 0, :], in_=src_halves[:, :, 1, :])
-            nc.vector.tensor_copy(out=dst_halves[:, :, 1, :], in_=src_halves[:, :, 0, :])
-
-        exchange_halves(w_words_swapped[:], w_words[:, 0 : 2 * QK])
-        exchange_halves(w_scales_swapped[:], w_scales[:, 0:QK])
-
+        nc.vector.tensor_copy(out=tables[:, 1, :, 0:HALF], in_=sin_rows[:, :, HALF:HEAD])
         nc.vector.tensor_scalar(
-            out=tables[:, 1, :, 0:HALF],
-            in0=tables[:, 1, :, 0:HALF],
+            out=tables[:, 1, :, HALF:HEAD],
+            in0=sin_rows[:, :, 0:HALF],
             scalar1=-1.0,
             scalar2=None,
             op0=MULT,
@@ -137,27 +126,22 @@ def tile_attention_pa_t_kernel(
             code_tiles[g], scale_tiles[g] = codes, scales
 
         def project(g):
-            v_bank = v_psum.tile([P, TILES, V], F32)
-            qk_banks[g] = []
-            for t in range(TILES):
-                tokens = slice(P * t, P * (t + 1))
-                qk_bank = qk_psum.tile([P, 2 * QK], F32)
-
-                def multiply(out, words, scales):
+            q_bank = qkv_psum.tile([P, TILES, V], F32)
+            k_bank = qkv_psum.tile([P, TILES, V], F32)
+            v_bank = qkv_psum.tile([P, TILES, V], F32)
+            for n, bank in enumerate((q_bank, k_bank, v_bank)):
+                for t in range(TILES):
+                    tokens = slice(P * t, P * (t + 1))
                     nc.tensor.matmul_mx(
-                        out=out,
+                        out=bank[:, t, :],
                         lhsT=code_tiles[g][:, tokens].bitcast(FP8X4),
                         lhsT_scale=scale_tiles[g][:, tokens],
-                        rhs=words.bitcast(FP4X4),
-                        rhs_scale=scales,
+                        rhs=w_words[:, 2 * V * n : 2 * V * (n + 1)].bitcast(FP4X4),
+                        rhs_scale=w_scales[:, V * n : V * (n + 1)],
                         start=True,
                         stop=True,
                     )
-
-                multiply(qk_bank[:, 0:QK], w_words[:, 0 : 2 * QK], w_scales[:, 0:QK])
-                multiply(qk_bank[:, QK : 2 * QK], w_words_swapped[:], w_scales_swapped[:])
-                multiply(v_bank[:, t, :], w_words[:, 2 * QK :], w_scales[:, QK:])
-                qk_banks[g].append(qk_bank)
+            qk_banks[g] = (q_bank, k_bank)
             v_banks[g] = v_bank
 
         def store_v(g):
@@ -173,22 +157,34 @@ def tile_attention_pa_t_kernel(
                 transpose(g + TRANSPOSE_AHEAD)
                 regroup(g + TRANSPOSE_AHEAD)
 
-        def rotate(products, i, g, t):
-            j = where(g)[1] + t
+        def rotate(products, first, g, a, c):
+            j0 = where(g)[1]
             nc.vector.tensor_tensor(
-                out=products[:, i, :].rearrange("p (c h d) -> p c h d", c=2, h=QK_HEADS),
-                in0=qk_banks[g][t][:].rearrange("p (c h d) -> p c h d", c=2, h=QK_HEADS),
-                in1=tables[:, :, j, :].unsqueeze(2).to_broadcast([P, 2, QK_HEADS, HEAD]),
+                out=products[:, c, a, first : first + TILES, :].rearrange(
+                    "p t (g d) -> p t g d", d=HEAD
+                ),
+                in0=qk_banks[g][a][:].rearrange("p t (g d) -> p t g d", d=HEAD),
+                in1=tables[:, c, j0 : j0 + TILES, :]
+                .unsqueeze(2)
+                .to_broadcast([P, TILES, V // HEAD, HEAD]),
                 op=MULT,
             )
 
-        def add(engine, products, qk_out, first, last):
-            engine.tensor_tensor(
-                out=qk_out[:, :, first:last, :].rearrange("p a i n -> p i a n"),
-                in0=products[:, first:last, 0:QK].rearrange("p i (a n) -> p i a n", a=2),
-                in1=products[:, first:last, QK : 2 * QK].rearrange("p i (a n) -> p i a n", a=2),
-                op=ADD,
-            )
+        def add(engine, products, qk_out, region):
+            a0, a1, first, last = region
+
+            def half_of(tiles, half):
+                return tiles.rearrange("p a i (g two w) -> p a (i g) two w", two=2, w=HALF)[
+                    :, :, :, half, :
+                ]
+
+            for half in range(2):
+                engine.tensor_tensor(
+                    out=half_of(qk_out[:, a0:a1, first:last, :], half),
+                    in0=half_of(products[:, 0, a0:a1, first:last, :], half),
+                    in1=half_of(products[:, 1, a0:a1, first:last, :], 1 - half),
+                    op=ADD,
+                )
 
         def store_qk(groups, qk_out):
             for n, g in enumerate(groups):
@@ -208,20 +204,28 @@ def tile_attention_pa_t_kernel(
         waiting = None
         for r, groups in enumerate(rounds):
             following = rounds[r + 1] if r + 1 < len(rounds) else range(0)
-            tiles = [(g, t) for g in groups for t in range(TILES)]
-            count = len(tiles)
+            slots = [(n, g, a, c) for n, g in enumerate(groups) for a in range(2) for c in range(2)]
+            count = TILES * len(groups)
             early = count - (min(len(groups), max(len(following), 1)) * TILES - 2)
-            products = product_pool.tile([P, count, 2 * QK], F32)
+            if len(groups) == 1:
+                before, after = [(0, 1, 0, TILES)], [(1, 2, 0, TILES)]
+            elif early <= TILES:
+                before, after = [(0, 2, 0, early)], [(0, 2, early, count)]
+            else:
+                before, after = [(0, 2, 0, TILES), (0, 1, TILES, count)], [(1, 2, TILES, count)]
+            products = product_pool.tile([P, 2, 2, count, 2 * HEAD], F32)
             qk_out = out_pool.tile([P, 2, count, 2 * HEAD], F32)
-            for i, (g, t) in enumerate(tiles):
-                if t == 0:
+            for i, (n, g, a, c) in enumerate(slots):
+                if a == 0 and c == 0:
                     feed(g)
-                if i == count - 1:
-                    add(nc.vector, products, qk_out, 0, early)
+                if i == len(slots) - 1:
+                    for region in before:
+                        add(nc.vector, products, qk_out, region)
                     for ahead in following:
                         quantise(ahead)
-                rotate(products, i, g, t)
-            add(nc.gpsimd if len(following) > 0 else nc.vector, products, qk_out, early, count)
+                rotate(products, TILES * n, g, a, c)
+            for region in after:
+                add(nc.gpsimd if len(following) > 0 else nc.vector, products, qk_out, region)
             if waiting is not None:
                 store_qk(*waiting)
             waiting = (groups, qk_out)

@@ -26,8 +26,6 @@ GROUPS = BATCH * ROWS // TILES
 
 FLOPS = 2 * BATCH * SEQ * HID * (QK + V)
 
-TRANSPOSE_AHEAD = 3
-
 
 def tile_attention_pa_t_kernel(
     tc, hidden_states, cos, sin, w_qkv_words, w_qkv_scales, out_0, out_1, out_2
@@ -150,13 +148,6 @@ def tile_attention_pa_t_kernel(
             nc.scalar.copy(out=v_out[:], in_=v_banks[g][:])
             nc.sync.dma_start(out=v_hbm[b, :, j0 : j0 + TILES, :], in_=v_out[:])
 
-        def feed(g):
-            project(g)
-            store_v(g)
-            if g + TRANSPOSE_AHEAD < GROUPS:
-                transpose(g + TRANSPOSE_AHEAD)
-                regroup(g + TRANSPOSE_AHEAD)
-
         def rotate(products, first, g, a, c):
             j0 = where(g)[1]
             nc.vector.tensor_tensor(
@@ -186,47 +177,55 @@ def tile_attention_pa_t_kernel(
                     op=ADD,
                 )
 
-        def store_qk(groups, qk_out):
-            for n, g in enumerate(groups):
-                b, j0 = where(g)
-                tiles = slice(TILES * n, TILES * (n + 1))
-                nc.sync.dma_start(out=q_hbm[b, :, j0 : j0 + TILES, :], in_=qk_out[:, 0, tiles, :])
-                nc.sync.dma_start(out=k_hbm[b, :, j0 : j0 + TILES, :], in_=qk_out[:, 1, tiles, :])
+        def store_qk(groups, qk_out, first, last):
+            g = groups[first // TILES]
+            b, j0 = where(g)
+            rows = slice(j0 + first % TILES, j0 + first % TILES + last - first)
+            nc.sync.dma_start(out=q_hbm[b, :, rows, :], in_=qk_out[:, 0, first:last, :])
+            nc.sync.dma_start(out=k_hbm[b, :, rows, :], in_=qk_out[:, 1, first:last, :])
 
-        for g in range(TRANSPOSE_AHEAD):
+        rounds = [[0], [1]] + [[g, g + 1] for g in range(2, GROUPS, 2)]
+        for g in rounds[0]:
             transpose(g)
             regroup(g)
-        quantise(0)
-
-        rounds = [range(0, 1)]
-        rounds += [range(g, g + 2) for g in range(1, GROUPS - 1, 2)]
-        rounds += [range(GROUPS - 1, GROUPS)]
+            quantise(g)
         waiting = None
         for r, groups in enumerate(rounds):
-            following = rounds[r + 1] if r + 1 < len(rounds) else range(0)
-            slots = [(n, g, a, c) for n, g in enumerate(groups) for a in range(2) for c in range(2)]
+            following = rounds[r + 1] if r + 1 < len(rounds) else []
             count = TILES * len(groups)
-            early = count - (min(len(groups), max(len(following), 1)) * TILES - 2)
-            if len(groups) == 1:
-                before, after = [(0, 1, 0, TILES)], [(1, 2, 0, TILES)]
-            elif early <= TILES:
-                before, after = [(0, 2, 0, early)], [(0, 2, early, count)]
+            if len(following) == 0:
+                before, after = [], [(0, 2, 0, TILES), (0, 2, TILES, count - 2), (0, 2, count - 2, count)]
+            elif TILES * len(following) > count:
+                before, after = [], [(0, 2, 0, count)]
+            elif len(groups) == 1:
+                before, after = [(0, 1, 0, 2)], [(0, 1, 2, count), (1, 2, 0, count)]
             else:
-                before, after = [(0, 2, 0, TILES), (0, 1, TILES, count)], [(1, 2, TILES, count)]
+                before, after = [(0, 2, 0, 1)], [(0, 2, 1, count)]
+            for g in following:
+                transpose(g)
+                regroup(g)
+            for g in groups:
+                project(g)
+                store_v(g)
             products = product_pool.tile([P, 2, 2, count, 2 * HEAD], F32)
             qk_out = out_pool.tile([P, 2, count, 2 * HEAD], F32)
-            for i, (n, g, a, c) in enumerate(slots):
-                if a == 0 and c == 0:
-                    feed(g)
-                if i == len(slots) - 1:
-                    for region in before:
-                        add(nc.vector, products, qk_out, region)
-                    for ahead in following:
-                        quantise(ahead)
+            slots = [(n, g, a, c) for n, g in enumerate(groups) for a in range(2) for c in range(2)]
+            for n, g, a, c in slots[:-1]:
                 rotate(products, TILES * n, g, a, c)
-            for region in after:
-                add(nc.gpsimd if len(following) > 0 else nc.vector, products, qk_out, region)
+            for region in before:
+                add(nc.vector, products, qk_out, region)
+            for g in following:
+                quantise(g)
+            n, g, a, c = slots[-1]
+            rotate(products, TILES * n, g, a, c)
             if waiting is not None:
-                store_qk(*waiting)
-            waiting = (groups, qk_out)
-        store_qk(*waiting)
+                for first in range(0, TILES * len(waiting[0]), TILES):
+                    store_qk(waiting[0], waiting[1], first, first + TILES)
+            if len(following) > 0:
+                for region in after:
+                    add(nc.gpsimd, products, qk_out, region)
+                waiting = (groups, qk_out)
+            else:
+                for region in after:
+                    add(nc.vector, products, qk_out, region)
+                    store_qk(groups, qk_out, region[2], region[3])

@@ -22,7 +22,8 @@ QK = QK_HEADS * HEAD
 V = 2 * HEAD
 ROWS = SEQ // P
 TILES = 4
-GROUPS = BATCH * ROWS // TILES
+GROUP_TILES = [2, 2] + [TILES] * (BATCH * ROWS // TILES - 1)
+GROUPS = len(GROUP_TILES)
 
 FLOPS = 2 * BATCH * SEQ * HID * (QK + V)
 
@@ -51,12 +52,13 @@ def tile_attention_pa_t_kernel(
         qk_banks, v_banks = {}, {}
 
         def where(g):
-            return g // (ROWS // TILES), TILES * (g % (ROWS // TILES))
+            first = sum(GROUP_TILES[:g])
+            return first // ROWS, first % ROWS, GROUP_TILES[g]
 
         def load(g):
-            b, j0 = where(g)
-            x_tile = x_pool.tile([P, TILES, HID], BF16)
-            nc.sync.dma_start(out=x_tile[:], in_=x_hbm[b, :, j0 : j0 + TILES, :])
+            b, j0, n = where(g)
+            x_tile = x_pool.tile([P, n, HID], BF16)
+            nc.sync.dma_start(out=x_tile[:], in_=x_hbm[b, :, j0 : j0 + n, :])
             x_tiles[g] = x_tile
 
         identity = consts.tile([P, P], F32)
@@ -75,9 +77,10 @@ def tile_attention_pa_t_kernel(
                 out=w_scales[32 * quadrant : 32 * quadrant + 4, :].bitcast(I32),
                 in_=w_qkv_scales[0, 4 * quadrant : 4 * quadrant + 4, :].bitcast(I32),
             )
+        load(1)
         nc.sync.dma_start(out=tables[:, 0, :, :], in_=cos.rearrange("(p j) d -> p j d", j=ROWS))
         nc.sync.dma_start(out=sin_rows[:], in_=sin.rearrange("(p j) d -> p j d", j=ROWS))
-        for g in range(1, GROUPS):
+        for g in range(2, GROUPS):
             load(g)
 
         nc.vector.tensor_copy(out=tables[:, 1, :, 0:HALF], in_=sin_rows[:, :, HALF:HEAD])
@@ -92,7 +95,7 @@ def tile_attention_pa_t_kernel(
         def transpose(g):
             x_words = x_tiles[g][:].bitcast(F32)
             xt_tiles[g] = []
-            for pair in range(TILES // 2):
+            for pair in range(GROUP_TILES[g] // 2):
                 x_transposed = xt_psum.tile([P, 2, 2, P], F32)
                 for t in range(2):
                     for u in range(2):
@@ -104,11 +107,10 @@ def tile_attention_pa_t_kernel(
                 xt_tiles[g].append(x_transposed)
 
         def regroup(g):
-            grouped = grouped_pool.tile([P, TILES * P * 4], BF16, align_bytes=64)
-            grouped_words = grouped[:].bitcast(F32).rearrange(
-                "p (t r u) -> p t r u", t=TILES, u=2
-            )
-            for pair in range(TILES // 2):
+            n = GROUP_TILES[g]
+            grouped = grouped_pool.tile([P, n * P * 4], BF16, align_bytes=64)
+            grouped_words = grouped[:].bitcast(F32).rearrange("p (t r u) -> p t r u", t=n, u=2)
+            for pair in range(n // 2):
                 nc.scalar.copy(
                     out=grouped_words[:, 2 * pair : 2 * pair + 2, :, :],
                     in_=xt_tiles[g][pair][:].rearrange("p t u r -> p t r u"),
@@ -116,19 +118,19 @@ def tile_attention_pa_t_kernel(
             grouped_tiles[g] = grouped
 
         def quantise(g):
-            codes = mx_pool.tile([P, TILES * P], U32, align_bytes=64)
-            scales = mx_pool.tile([P, TILES * P], U8, align_bytes=64)
+            codes = mx_pool.tile([P, GROUP_TILES[g] * P], U32, align_bytes=64)
+            scales = mx_pool.tile([P, GROUP_TILES[g] * P], U8, align_bytes=64)
             nc.vector.quantize_mx(
                 out=codes[:].bitcast(FP8X4), scales=scales[:], in_=grouped_tiles[g][:]
             )
             code_tiles[g], scale_tiles[g] = codes, scales
 
         def project(g):
-            q_bank = qkv_psum.tile([P, TILES, V], F32)
-            k_bank = qkv_psum.tile([P, TILES, V], F32)
-            v_bank = qkv_psum.tile([P, TILES, V], F32)
+            q_bank = qkv_psum.tile([P, GROUP_TILES[g], V], F32)
+            k_bank = qkv_psum.tile([P, GROUP_TILES[g], V], F32)
+            v_bank = qkv_psum.tile([P, GROUP_TILES[g], V], F32)
             for n, bank in enumerate((q_bank, k_bank, v_bank)):
-                for t in range(TILES):
+                for t in range(GROUP_TILES[g]):
                     tokens = slice(P * t, P * (t + 1))
                     nc.tensor.matmul_mx(
                         out=bank[:, t, :],
@@ -143,21 +145,19 @@ def tile_attention_pa_t_kernel(
             v_banks[g] = v_bank
 
         def store_v(g):
-            b, j0 = where(g)
-            v_out = out_pool.tile([P, TILES, V], F32)
+            b, j0, n = where(g)
+            v_out = out_pool.tile([P, n, V], F32)
             nc.scalar.copy(out=v_out[:], in_=v_banks[g][:])
-            nc.sync.dma_start(out=v_hbm[b, :, j0 : j0 + TILES, :], in_=v_out[:])
+            nc.sync.dma_start(out=v_hbm[b, :, j0 : j0 + n, :], in_=v_out[:])
 
         def rotate(products, first, g, a, c):
-            j0 = where(g)[1]
+            b, j0, n = where(g)
             nc.vector.tensor_tensor(
-                out=products[:, c, a, first : first + TILES, :].rearrange(
+                out=products[:, c, a, first : first + n, :].rearrange(
                     "p t (g d) -> p t g d", d=HEAD
                 ),
                 in0=qk_banks[g][a][:].rearrange("p t (g d) -> p t g d", d=HEAD),
-                in1=tables[:, c, j0 : j0 + TILES, :]
-                .unsqueeze(2)
-                .to_broadcast([P, TILES, V // HEAD, HEAD]),
+                in1=tables[:, c, j0 : j0 + n, :].unsqueeze(2).to_broadcast([P, n, V // HEAD, HEAD]),
                 op=MULT,
             )
 
@@ -178,13 +178,12 @@ def tile_attention_pa_t_kernel(
                 )
 
         def store_qk(groups, qk_out, first, last):
-            g = groups[first // TILES]
-            b, j0 = where(g)
-            rows = slice(j0 + first % TILES, j0 + first % TILES + last - first)
+            b, j0, n = where(groups[0])
+            rows = slice(j0 + first, j0 + last)
             nc.sync.dma_start(out=q_hbm[b, :, rows, :], in_=qk_out[:, 0, first:last, :])
             nc.sync.dma_start(out=k_hbm[b, :, rows, :], in_=qk_out[:, 1, first:last, :])
 
-        rounds = [[0], [1]] + [[g, g + 1] for g in range(2, GROUPS, 2)]
+        rounds = [[0], [1], [2]] + [[g, g + 1] for g in range(3, GROUPS, 2)]
         for g in rounds[0]:
             transpose(g)
             regroup(g)
@@ -192,39 +191,47 @@ def tile_attention_pa_t_kernel(
         waiting = None
         for r, groups in enumerate(rounds):
             following = rounds[r + 1] if r + 1 < len(rounds) else []
-            count = TILES * len(groups)
+            count = sum(GROUP_TILES[g] for g in groups)
             if len(following) == 0:
                 before, after = [], [(0, 2, 0, TILES), (0, 2, TILES, count - 2), (0, 2, count - 2, count)]
-            elif TILES * len(following) > count:
+            elif sum(GROUP_TILES[g] for g in following) > count:
                 before, after = [], [(0, 2, 0, count)]
             elif len(groups) == 1:
-                before, after = [(0, 1, 0, 2)], [(0, 1, 2, count), (1, 2, 0, count)]
+                before, after = [(0, 1, 0, 1)], [(0, 1, 1, count), (1, 2, 0, count)]
             else:
-                before, after = [(0, 2, 0, 1)], [(0, 2, 1, count)]
-            for g in following:
+                before, after = [(0, 2, 0, 2)], [(0, 2, 2, count)]
+            for g in following[:1]:
                 transpose(g)
                 regroup(g)
             for g in groups:
                 project(g)
                 store_v(g)
+            for g in following[1:]:
+                transpose(g)
+                regroup(g)
             products = product_pool.tile([P, 2, 2, count, 2 * HEAD], F32)
             qk_out = out_pool.tile([P, 2, count, 2 * HEAD], F32)
-            slots = [(n, g, a, c) for n, g in enumerate(groups) for a in range(2) for c in range(2)]
-            for n, g, a, c in slots[:-1]:
-                rotate(products, TILES * n, g, a, c)
+            slots = [
+                (sum(GROUP_TILES[m] for m in groups[:n]), g, a, c)
+                for n, g in enumerate(groups)
+                for a in range(2)
+                for c in range(2)
+            ]
+            for first, g, a, c in slots[:-1]:
+                rotate(products, first, g, a, c)
             for region in before:
                 add(nc.vector, products, qk_out, region)
             for g in following:
                 quantise(g)
-            n, g, a, c = slots[-1]
-            rotate(products, TILES * n, g, a, c)
+            first, g, a, c = slots[-1]
+            rotate(products, first, g, a, c)
             if waiting is not None:
-                for first in range(0, TILES * len(waiting[0]), TILES):
-                    store_qk(waiting[0], waiting[1], first, first + TILES)
+                for first in range(0, waiting[2], TILES):
+                    store_qk(waiting[0], waiting[1], first, min(first + TILES, waiting[2]))
             if len(following) > 0:
                 for region in after:
                     add(nc.gpsimd, products, qk_out, region)
-                waiting = (groups, qk_out)
+                waiting = (groups, qk_out, count)
             else:
                 for region in after:
                     add(nc.vector, products, qk_out, region)

@@ -68,7 +68,6 @@ def tile_attention_pa_t_kernel(
         w_scales = consts.tile([P, QK + V], U8, align_bytes=64)
         nc.vector.memset(w_scales[:].bitcast(I32), 0)
         tables = consts.tile([P, 2, ROWS, HEAD], BF16)
-        sin_rows = consts.tile([P, ROWS, HEAD], BF16)
 
         load(0)
         nc.sync.dma_start(out=w_words[:].bitcast(I32), in_=w_qkv_words[0].bitcast(I32))
@@ -79,14 +78,13 @@ def tile_attention_pa_t_kernel(
             )
         load(1)
         nc.sync.dma_start(out=tables[:, 0, :, :], in_=cos.rearrange("(p j) d -> p j d", j=ROWS))
-        nc.sync.dma_start(out=sin_rows[:], in_=sin.rearrange("(p j) d -> p j d", j=ROWS))
+        nc.sync.dma_start(out=tables[:, 1, :, :], in_=sin.rearrange("(p j) d -> p j d", j=ROWS))
         for g in range(2, GROUPS):
             load(g)
 
-        nc.vector.tensor_copy(out=tables[:, 1, :, 0:HALF], in_=sin_rows[:, :, HALF:HEAD])
         nc.vector.tensor_scalar(
-            out=tables[:, 1, :, HALF:HEAD],
-            in0=sin_rows[:, :, 0:HALF],
+            out=tables[:, 1, :, 0:HALF],
+            in0=tables[:, 1, :, 0:HALF],
             scalar1=-1.0,
             scalar2=None,
             op0=MULT,
@@ -152,30 +150,27 @@ def tile_attention_pa_t_kernel(
 
         def rotate(products, first, g, a, c):
             b, j0, n = where(g)
+            halves = qk_banks[g][a][:].rearrange("p t (g two w) -> p t g two w", two=2, w=HALF)
             nc.vector.tensor_tensor(
                 out=products[:, c, a, first : first + n, :].rearrange(
-                    "p t (g d) -> p t g d", d=HEAD
+                    "p t (g two w) -> p t g two w", two=2, w=HALF
                 ),
-                in0=qk_banks[g][a][:].rearrange("p t (g d) -> p t g d", d=HEAD),
-                in1=tables[:, c, j0 : j0 + n, :].unsqueeze(2).to_broadcast([P, n, V // HEAD, HEAD]),
+                in0=halves if c == 0 else halves[:, :, :, ::-1, :],
+                in1=tables[:, c, j0 : j0 + n, :]
+                .rearrange("p t (two w) -> p t two w", two=2)
+                .unsqueeze(2)
+                .to_broadcast([P, n, V // HEAD, 2, HALF]),
                 op=MULT,
             )
 
         def add(engine, products, qk_out, region):
             a0, a1, first, last = region
-
-            def half_of(tiles, half):
-                return tiles.rearrange("p a i (g two w) -> p a (i g) two w", two=2, w=HALF)[
-                    :, :, :, half, :
-                ]
-
-            for half in range(2):
-                engine.tensor_tensor(
-                    out=half_of(qk_out[:, a0:a1, first:last, :], half),
-                    in0=half_of(products[:, 0, a0:a1, first:last, :], half),
-                    in1=half_of(products[:, 1, a0:a1, first:last, :], 1 - half),
-                    op=ADD,
-                )
+            engine.tensor_tensor(
+                out=qk_out[:, a0:a1, first:last, :],
+                in0=products[:, 0, a0:a1, first:last, :],
+                in1=products[:, 1, a0:a1, first:last, :],
+                op=ADD,
+            )
 
         def store_qk(groups, qk_out, first, last):
             b, j0, n = where(groups[0])

@@ -40,8 +40,8 @@ def tile_attention_pa_t_kernel(
     with ExitStack() as stack:
         consts = stack.enter_context(tc.tile_pool(name="consts", bufs=1))
         x_pool = stack.enter_context(tc.tile_pool(name="x", bufs=GROUPS))
-        grouped_pool = stack.enter_context(tc.tile_pool(name="grouped", bufs=4))
-        mx_pool = stack.enter_context(tc.tile_pool(name="mx", bufs=4))
+        grouped_pool = stack.enter_context(tc.tile_pool(name="grouped", bufs=5))
+        mx_pool = stack.enter_context(tc.tile_pool(name="mx", bufs=6))
         product_pool = stack.enter_context(tc.tile_pool(name="products", bufs=3))
         out_pool = stack.enter_context(tc.tile_pool(name="outputs", bufs=6))
         xt_psum = stack.enter_context(tc.psum_pool(name="xt", bufs=2))
@@ -179,31 +179,40 @@ def tile_attention_pa_t_kernel(
             nc.sync.dma_start(out=k_hbm[b, :, rows, :], in_=qk_out[:, 1, first:last, :])
 
         rounds = [[0], [1], [2]] + [[g, g + 1] for g in range(3, GROUPS, 2)]
-        for g in rounds[0]:
+        ahead = [[1], [2], [3, 4], [5, 6, 7]] + [
+            [g for g in (groups[-1] + 2, groups[-1] + 3) if g < GROUPS] for groups in rounds[4:]
+        ]
+        rotated, quantised, projected = [], [], []
+
+        def project_what_can_be():
+            while (
+                len(projected) < GROUPS
+                and len(projected) in quantised
+                and (len(projected) < 2 or len(projected) - 2 in rotated)
+            ):
+                project(len(projected))
+                store_v(len(projected))
+                projected.append(len(projected))
+
+        for g in [0] + ahead[0]:
             transpose(g)
             regroup(g)
-            quantise(g)
+        quantise(0)
+        quantised.append(0)
+        project_what_can_be()
         waiting = None
         for r, groups in enumerate(rounds):
-            following = rounds[r + 1] if r + 1 < len(rounds) else []
+            last_round = r + 1 == len(rounds)
             count = sum(GROUP_TILES[g] for g in groups)
-            if len(following) == 0:
+            if last_round:
                 before, after = [], [(0, 2, 0, TILES), (0, 2, TILES, count - 2), (0, 2, count - 2, count)]
-            elif sum(GROUP_TILES[g] for g in following) > count:
+            elif sum(GROUP_TILES[g] for g in rounds[r + 1]) > count:
                 before, after = [], [(0, 2, 0, count)]
             elif len(groups) == 1:
                 before, after = [(0, 1, 0, 1)], [(0, 1, 1, count), (1, 2, 0, count)]
             else:
                 before, after = [(0, 2, 0, 2)], [(0, 2, 2, count)]
-            for g in following[:1]:
-                transpose(g)
-                regroup(g)
-            for g in groups:
-                project(g)
-                store_v(g)
-            for g in following[1:]:
-                transpose(g)
-                regroup(g)
+            to_transpose = ahead[r + 1] if not last_round else []
             products = product_pool.tile([P, 2, 2, count, 2 * HEAD], F32)
             qk_out = out_pool.tile([P, 2, count, 2 * HEAD], F32)
             slots = [
@@ -214,16 +223,28 @@ def tile_attention_pa_t_kernel(
             ]
             for first, g, a, c in slots[:-1]:
                 rotate(products, first, g, a, c)
-            for region in before:
-                add(nc.vector, products, qk_out, region)
-            for g in following:
-                quantise(g)
-            first, g, a, c = slots[-1]
-            rotate(products, first, g, a, c)
+                if a == 1 and c == 1:
+                    rotated.append(g)
+                    project_what_can_be()
             if waiting is not None:
                 for first in range(0, waiting[2], TILES):
                     store_qk(waiting[0], waiting[1], first, min(first + TILES, waiting[2]))
-            if len(following) > 0:
+            for g in to_transpose[:1]:
+                transpose(g)
+                regroup(g)
+            for region in before:
+                add(nc.vector, products, qk_out, region)
+            for g in ahead[r]:
+                quantise(g)
+                quantised.append(g)
+            first, g, a, c = slots[-1]
+            rotate(products, first, g, a, c)
+            rotated.append(g)
+            project_what_can_be()
+            for g in to_transpose[1:]:
+                transpose(g)
+                regroup(g)
+            if not last_round:
                 for region in after:
                     add(nc.gpsimd, products, qk_out, region)
                 waiting = (groups, qk_out, count)

@@ -148,9 +148,13 @@ def tile_attention_pa_t_kernel(
             nc.scalar.copy(out=v_out[:], in_=v_banks[g][:])
             nc.sync.dma_start(out=v_hbm[b, :, j0 : j0 + n, :], in_=v_out[:])
 
-        def rotate(products, first, g, a, c):
+        def rotate(products, first, g, a, c, t0=0, t1=None):
             b, j0, n = where(g)
-            halves = qk_banks[g][a][:].rearrange("p t (g two w) -> p t g two w", two=2, w=HALF)
+            t1 = n if t1 is None else t1
+            first, j0, n = first + t0, j0 + t0, t1 - t0
+            halves = qk_banks[g][a][:, t0:t1, :].rearrange(
+                "p t (g two w) -> p t g two w", two=2, w=HALF
+            )
             nc.vector.tensor_tensor(
                 out=products[:, c, a, first : first + n, :].rearrange(
                     "p t (g two w) -> p t g two w", two=2, w=HALF
@@ -205,13 +209,15 @@ def tile_attention_pa_t_kernel(
             last_round = r + 1 == len(rounds)
             count = sum(GROUP_TILES[g] for g in groups)
             if last_round:
-                before, after = [], [(0, 2, 0, TILES), (0, 2, TILES, count - 2), (0, 2, count - 2, count)]
+                before, after = [(0, 2, 0, TILES)], [(0, 2, TILES, count - 2), (0, 2, count - 2, count)]
             elif sum(GROUP_TILES[g] for g in rounds[r + 1]) > count:
                 before, after = [], [(0, 2, 0, count)]
             elif len(groups) == 1:
                 before, after = [(0, 1, 0, 1)], [(0, 1, 1, count), (1, 2, 0, count)]
+            elif r + 2 == len(rounds):
+                before, after = [(0, 2, 0, 1)], [(0, 2, 1, TILES), (0, 2, TILES, count)]
             else:
-                before, after = [(0, 2, 0, 2)], [(0, 2, 2, count)]
+                before, after = [(0, 2, 0, 1)], [(0, 2, 1, count)]
             to_transpose = ahead[r + 1] if not last_round else []
             products = product_pool.tile([P, 2, 2, count, 2 * HEAD], F32)
             qk_out = out_pool.tile([P, 2, count, 2 * HEAD], F32)
@@ -221,11 +227,15 @@ def tile_attention_pa_t_kernel(
                 for a in range(2)
                 for c in range(2)
             ]
-            for first, g, a, c in slots[:-1]:
+            late = 2 if last_round else 1
+            for first, g, a, c in slots[:-late]:
                 rotate(products, first, g, a, c)
                 if a == 1 and c == 1:
                     rotated.append(g)
                     project_what_can_be()
+            if not last_round:
+                first, g, a, c = slots[-1]
+                rotate(products, first, g, a, c, 0, GROUP_TILES[g] - 1)
             if waiting is not None:
                 for first in range(0, waiting[2], TILES):
                     store_qk(waiting[0], waiting[1], first, min(first + TILES, waiting[2]))
@@ -234,11 +244,13 @@ def tile_attention_pa_t_kernel(
                 regroup(g)
             for region in before:
                 add(nc.vector, products, qk_out, region)
+                if last_round:
+                    store_qk(groups, qk_out, region[2], region[3])
             for g in ahead[r]:
                 quantise(g)
                 quantised.append(g)
-            first, g, a, c = slots[-1]
-            rotate(products, first, g, a, c)
+            for first, g, a, c in slots[-late:]:
+                rotate(products, first, g, a, c, 0 if last_round else GROUP_TILES[g] - 1)
             rotated.append(g)
             project_what_can_be()
             for g in to_transpose[1:]:

from contextlib import ExitStack

import concourse.mybir as mybir
from concourse.masks import make_identity

F32 = mybir.dt.float32
BF16 = mybir.dt.bfloat16
I32 = mybir.dt.int32
U32 = mybir.dt.uint32
U8 = mybir.dt.uint8
FP8X4 = mybir.dt.float8_e4m3fn_x4
FP4X4 = mybir.dt.float4_e2m1fn_x4
MULT = mybir.AluOpType.mult
ADD = mybir.AluOpType.add

P = 128
BATCH, SEQ, HID = 4, 2048, 512
HEAD = 64
HALF = HEAD // 2
QK_HEADS = 4
QK = QK_HEADS * HEAD
V = 2 * HEAD
ROWS = SEQ // P
TILES = 4
GROUP_TILES = [2, 2] + [TILES] * (BATCH * ROWS // TILES - 1)
GROUPS = len(GROUP_TILES)

FLOPS = 2 * BATCH * SEQ * HID * (QK + V)


def tile_attention_pa_t_kernel(
    tc, hidden_states, cos, sin, w_qkv_words, w_qkv_scales, out_0, out_1, out_2
):
    nc = tc.nc
    x_hbm = hidden_states.rearrange("b (p j) k -> b p j k", j=ROWS)
    q_hbm = out_0.rearrange("b (p j) h d -> b p j (h d)", j=ROWS)
    k_hbm = out_1.rearrange("b (p j) h d -> b p j (h d)", j=ROWS)
    v_hbm = out_2.rearrange("b (p j) h d -> b p j (h d)", j=ROWS)

    with ExitStack() as stack:
        consts = stack.enter_context(tc.tile_pool(name="consts", bufs=1))
        x_pool = stack.enter_context(tc.tile_pool(name="x", bufs=GROUPS))
        grouped_pool = stack.enter_context(tc.tile_pool(name="grouped", bufs=5))
        mx_pool = stack.enter_context(tc.tile_pool(name="mx", bufs=6))
        product_pool = stack.enter_context(tc.tile_pool(name="products", bufs=3))
        out_pool = stack.enter_context(tc.tile_pool(name="outputs", bufs=6))
        xt_psum = stack.enter_context(tc.psum_pool(name="xt", bufs=2))
        qkv_psum = stack.enter_context(tc.psum_pool(name="qkv", bufs=2))
        stack.enter_context(tc.manual_schedule())

        x_tiles, xt_tiles, grouped_tiles, code_tiles, scale_tiles = {}, {}, {}, {}, {}
        qk_banks, v_banks = {}, {}

        def where(g):
            first = sum(GROUP_TILES[:g])
            return first // ROWS, first % ROWS, GROUP_TILES[g]

        def load(g):
            b, j0, n = where(g)
            x_tile = x_pool.tile([P, n, HID], BF16)
            nc.sync.dma_start(out=x_tile[:], in_=x_hbm[b, :, j0 : j0 + n, :])
            x_tiles[g] = x_tile

        identity = consts.tile([P, P], F32)
        make_identity(nc, identity[:])

        w_words = consts.tile([P, 2 * (QK + V)], U8, align_bytes=64)
        w_scales = consts.tile([P, QK + V], U8, align_bytes=64)
        nc.vector.memset(w_scales[:].bitcast(I32), 0)
        tables = consts.tile([P, 2, ROWS, HEAD], BF16)

        load(0)
        nc.sync.dma_start(out=w_words[:].bitcast(I32), in_=w_qkv_words[0].bitcast(I32))
        for quadrant in range(4):
            nc.sync.dma_start(
                out=w_scales[32 * quadrant : 32 * quadrant + 4, :].bitcast(I32),
                in_=w_qkv_scales[0, 4 * quadrant : 4 * quadrant + 4, :].bitcast(I32),
            )
        load(1)
        nc.sync.dma_start(out=tables[:, 0, :, :], in_=cos.rearrange("(p j) d -> p j d", j=ROWS))
        nc.sync.dma_start(out=tables[:, 1, :, :], in_=sin.rearrange("(p j) d -> p j d", j=ROWS))
        for g in range(2, GROUPS):
            load(g)

        nc.vector.tensor_scalar(
            out=tables[:, 1, :, 0:HALF],
            in0=tables[:, 1, :, 0:HALF],
            scalar1=-1.0,
            scalar2=None,
            op0=MULT,
        )

        def transpose(g):
            x_words = x_tiles[g][:].bitcast(F32)
            xt_tiles[g] = []
            for pair in range(GROUP_TILES[g] // 2):
                x_transposed = xt_psum.tile([P, 2, 2, P], F32)
                for t in range(2):
                    for u in range(2):
                        nc.tensor.transpose(
                            x_transposed[:, t, u, :],
                            x_words[:, 2 * pair + t, u : HID // 2 : 2],
                            identity[:],
                        )
                xt_tiles[g].append(x_transposed)

        def regroup(g):
            n = GROUP_TILES[g]
            grouped = grouped_pool.tile([P, n * P * 4], BF16, align_bytes=64)
            grouped_words = grouped[:].bitcast(F32).rearrange("p (t r u) -> p t r u", t=n, u=2)
            for pair in range(n // 2):
                nc.scalar.copy(
                    out=grouped_words[:, 2 * pair : 2 * pair + 2, :, :],
                    in_=xt_tiles[g][pair][:].rearrange("p t u r -> p t r u"),
                )
            grouped_tiles[g] = grouped

        def quantise(g):
            codes = mx_pool.tile([P, GROUP_TILES[g] * P], U32, align_bytes=64)
            scales = mx_pool.tile([P, GROUP_TILES[g] * P], U8, align_bytes=64)
            nc.vector.quantize_mx(
                out=codes[:].bitcast(FP8X4), scales=scales[:], in_=grouped_tiles[g][:]
            )
            code_tiles[g], scale_tiles[g] = codes, scales

        def project(g):
            q_bank = qkv_psum.tile([P, GROUP_TILES[g], V], F32)
            k_bank = qkv_psum.tile([P, GROUP_TILES[g], V], F32)
            v_bank = qkv_psum.tile([P, GROUP_TILES[g], V], F32)
            for n, bank in enumerate((q_bank, k_bank, v_bank)):
                for t in range(GROUP_TILES[g]):
                    tokens = slice(P * t, P * (t + 1))
                    nc.tensor.matmul_mx(
                        out=bank[:, t, :],
                        lhsT=code_tiles[g][:, tokens].bitcast(FP8X4),
                        lhsT_scale=scale_tiles[g][:, tokens],
                        rhs=w_words[:, 2 * V * n : 2 * V * (n + 1)].bitcast(FP4X4),
                        rhs_scale=w_scales[:, V * n : V * (n + 1)],
                        start=True,
                        stop=True,
                    )
            qk_banks[g] = (q_bank, k_bank)
            v_banks[g] = v_bank

        def store_v(g):
            b, j0, n = where(g)
            v_out = out_pool.tile([P, n, V], F32)
            nc.scalar.copy(out=v_out[:], in_=v_banks[g][:])
            nc.sync.dma_start(out=v_hbm[b, :, j0 : j0 + n, :], in_=v_out[:])

        def rotate(products, first, g, a, c, t0=0, t1=None):
            b, j0, n = where(g)
            t1 = n if t1 is None else t1
            first, j0, n = first + t0, j0 + t0, t1 - t0
            halves = qk_banks[g][a][:, t0:t1, :].rearrange(
                "p t (g two w) -> p t g two w", two=2, w=HALF
            )
            nc.vector.tensor_tensor(
                out=products[:, c, a, first : first + n, :].rearrange(
                    "p t (g two w) -> p t g two w", two=2, w=HALF
                ),
                in0=halves if c == 0 else halves[:, :, :, ::-1, :],
                in1=tables[:, c, j0 : j0 + n, :]
                .rearrange("p t (two w) -> p t two w", two=2)
                .unsqueeze(2)
                .to_broadcast([P, n, V // HEAD, 2, HALF]),
                op=MULT,
            )

        def add(engine, products, qk_out, region):
            a0, a1, first, last = region
            engine.tensor_tensor(
                out=qk_out[:, a0:a1, first:last, :],
                in0=products[:, 0, a0:a1, first:last, :],
                in1=products[:, 1, a0:a1, first:last, :],
                op=ADD,
            )

        def store_qk(groups, qk_out, first, last):
            b, j0, n = where(groups[0])
            rows = slice(j0 + first, j0 + last)
            nc.sync.dma_start(out=q_hbm[b, :, rows, :], in_=qk_out[:, 0, first:last, :])
            nc.sync.dma_start(out=k_hbm[b, :, rows, :], in_=qk_out[:, 1, first:last, :])

        rounds = [[0], [1], [2]] + [[g, g + 1] for g in range(3, GROUPS, 2)]
        ahead = [[1], [2], [3, 4], [5, 6, 7]] + [
            [g for g in (groups[-1] + 2, groups[-1] + 3) if g < GROUPS] for groups in rounds[4:]
        ]
        rotated, quantised, projected = [], [], []

        def project_what_can_be():
            while (
                len(projected) < GROUPS
                and len(projected) in quantised
                and (len(projected) < 2 or len(projected) - 2 in rotated)
            ):
                project(len(projected))
                store_v(len(projected))
                projected.append(len(projected))

        for g in [0] + ahead[0]:
            transpose(g)
            regroup(g)
        quantise(0)
        quantised.append(0)
        project_what_can_be()
        waiting = None
        for r, groups in enumerate(rounds):
            last_round = r + 1 == len(rounds)
            count = sum(GROUP_TILES[g] for g in groups)
            if last_round:
                before, after = [(0, 2, 0, TILES)], [(0, 2, TILES, count - 2), (0, 2, count - 2, count)]
            elif sum(GROUP_TILES[g] for g in rounds[r + 1]) > count:
                before, after = [], [(0, 2, 0, count)]
            elif len(groups) == 1:
                before, after = [(0, 1, 0, 1)], [(0, 1, 1, count), (1, 2, 0, count)]
            elif r + 2 == len(rounds):
                before, after = [(0, 2, 0, 1)], [(0, 2, 1, TILES), (0, 2, TILES, count)]
            else:
                before, after = [(0, 2, 0, 1)], [(0, 2, 1, count)]
            to_transpose = ahead[r + 1] if not last_round else []
            products = product_pool.tile([P, 2, 2, count, 2 * HEAD], F32)
            qk_out = out_pool.tile([P, 2, count, 2 * HEAD], F32)
            slots = [
                (sum(GROUP_TILES[m] for m in groups[:n]), g, a, c)
                for n, g in enumerate(groups)
                for a in range(2)
                for c in range(2)
            ]
            late = 2 if last_round else 1
            for first, g, a, c in slots[:-late]:
                rotate(products, first, g, a, c)
                if a == 1 and c == 1:
                    rotated.append(g)
                    project_what_can_be()
            if not last_round:
                first, g, a, c = slots[-1]
                rotate(products, first, g, a, c, 0, GROUP_TILES[g] - 1)
            if waiting is not None:
                for first in range(0, waiting[2], TILES):
                    store_qk(waiting[0], waiting[1], first, min(first + TILES, waiting[2]))
            for g in to_transpose[:1]:
                transpose(g)
                regroup(g)
            for region in before:
                add(nc.vector, products, qk_out, region)
                if last_round:
                    store_qk(groups, qk_out, region[2], region[3])
            for g in ahead[r]:
                quantise(g)
                quantised.append(g)
            for first, g, a, c in slots[-late:]:
                rotate(products, first, g, a, c, 0 if last_round else GROUP_TILES[g] - 1)
            rotated.append(g)
            project_what_can_be()
            for g in to_transpose[1:]:
                transpose(g)
                regroup(g)
            if not last_round:
                for region in after:
                    add(nc.gpsimd, products, qk_out, region)
                waiting = (groups, qk_out, count)
            else:
                for region in after:
                    add(nc.vector, products, qk_out, region)
                    store_qk(groups, qk_out, region[2], region[3])
